import numpy as np
import ml_dtypes


def mxq(x, axis, fmt="e4m3"):
    dtype, down = {"e4m3": (ml_dtypes.float8_e4m3fn, 7), "e5m2": (ml_dtypes.float8_e5m2, 14)}[fmt]
    v = np.moveaxis(np.asarray(x, np.float32).astype(ml_dtypes.bfloat16).astype(np.float64), axis, -1)
    blocks = v.reshape(v.shape[:-1] + (-1, 32))
    amax = np.abs(blocks).max(-1, keepdims=True)
    byte = np.maximum(np.where(amax > 0, np.frexp(amax)[1] - 1 + 127, 0) - down, 1)
    scale = np.exp2(byte - 127.0)
    codes = (blocks / scale).astype(np.float32).astype(dtype).astype(np.float64)
    return np.moveaxis((codes * scale).reshape(v.shape), -1, axis)


WIDE = False


def mx_kscale(k):
    if not WIDE:
        return np.ones(k)
    levels = np.array([10, -10, 5, -5, 0])
    a = np.random.permutation(np.resize(levels, k // 512 * 4)).reshape(k // 512, 4)
    idx = np.arange(k)
    return np.exp2(a[idx // 512, idx % 128 // 32])


BF16 = ml_dtypes.bfloat16


def bf(x):
    return np.asarray(x, np.float32).astype(BF16)


def f64(x):
    return np.asarray(x).astype(np.float64)


E2M1 = np.array([0.0, 0.5, 1.0, 1.5, 2.0, 3.0, 4.0, 6.0, -0.0, -0.5, -1.0, -1.5, -2.0, -3.0, -4.0, -6.0])


def pack_weight(w, fmt):
    k, n = w.shape
    w = f64(bf(w)).reshape(k // 32, 32, n)
    amax = np.abs(w).max(1)
    if fmt == "e4m3":
        byte = np.frexp(amax)[1] - 1 + 127 - 7
    else:
        mant, ex = np.frexp(amax / 6.0)
        byte = np.where(mant > 0.5, ex, ex - 1) + 127
    byte = np.clip(np.where(amax > 0, byte, 1), 1, 254)
    scaled = (w * np.exp2(127.0 - byte)[:, None, :]).reshape(k, n).astype(np.float32)
    by_word = np.ascontiguousarray(scaled.reshape(k // 512, 128, 4, n).transpose(0, 1, 3, 2))
    if fmt == "e4m3":
        words = by_word.astype(ml_dtypes.float8_e4m3fn).view(np.uint8)
    else:
        c = by_word.astype(ml_dtypes.float4_e2m1fn).view(np.uint8) & 0xF
        words = c[..., 0::2] | (c[..., 1::2] << 4)
    return np.ascontiguousarray(words), np.ascontiguousarray(byte.astype(np.uint8).reshape(k // 512, 16, n))


def unpack_weight(words, scales, fmt):
    g, p, n, _ = words.shape
    if fmt == "e4m3":
        vals = np.ascontiguousarray(words).view(ml_dtypes.float8_e4m3fn).astype(np.float64)
    else:
        nib = np.empty((g, p, n, 4), np.uint8)
        nib[..., 0::2] = words & 0xF
        nib[..., 1::2] = words >> 4
        vals = E2M1[nib]
    vals = vals * np.repeat(np.exp2(scales.astype(np.float64) - 127.0), 8, axis=1)[..., None]
    return vals.transpose(0, 1, 3, 2).reshape(g * 512, n)


G, S, M, H, E, C = 2, 512, 512, 1024, 16, 64


def setup_inputs():
    s, t = mx_kscale(S), mx_kscale(M)
    dispatch_mask = bf(np.random.standard_normal((G, S, E, C)) * 0.1 * s[None, :, None, None])
    x = bf(np.random.standard_normal((G, S, M)) / s[None, :, None] * t)
    wi = np.random.standard_normal((E, M, H)) * 10.0 / np.sqrt(S * M) / t[None, :, None]
    wi_words, wi_scales = pack_weight(wi.reshape(-1, H), "e4m3")
    return {"dispatch_mask": dispatch_mask,
            "x": x,
            "wi_words": wi_words,
            "wi_scales": wi_scales}


def reference(dispatch_mask, x, wi_words, wi_scales):
    dm = mxq(f64(dispatch_mask).reshape(G, S, E * C), 1, "e4m3")
    xq = mxq(f64(x), 1, "e4m3")
    d = dm.transpose(0, 2, 1) @ xq
    dispatched = d.reshape(G, E, C, M).transpose(1, 0, 2, 3)
    pre = mxq(dispatched.reshape(E, G * C, M), 2, "e4m3") @ unpack_weight(wi_words, wi_scales, "e4m3").reshape(E, M, H)
    return np.maximum(pre, 0.0).reshape(E, G, C, H)

@@ -1,0 +1,151 @@
+from contextlib import ExitStack
+
+import concourse.mybir as mybir
+
+BF16 = mybir.dt.bfloat16
+F32 = mybir.dt.float32
+I32 = mybir.dt.int32
+U32 = mybir.dt.uint32
+U8 = mybir.dt.uint8
+FP8X4 = mybir.dt.float8_e4m3fn_x4
+RELU = mybir.ActivationFunctionType.Relu
+
+G, S, M, H, E, C = 2, 512, 512, 1024, 16, 64
+P = 128
+PACK = 4
+SLOTS = E * C
+PAIR = 2
+N_PAIRS = E // PAIR
+BANK = 512
+PLANES = 4
+QUADRANTS = 4
+
+FLOPS = 2 * G * S * SLOTS * M + 2 * E * G * C * M * H
+
+
+def tile_flaxpositionwisemoelayer_pa_e_kernel(tc, dispatch_mask, x, wi_words, wi_scales, out):
+    nc = tc.nc
+    with ExitStack() as ctx:
+        keep = ctx.enter_context(tc.tile_pool(name="keep", bufs=1))
+        psum_d = ctx.enter_context(tc.psum_pool(name="psum_d", bufs=4))
+        psum_h = ctx.enter_context(tc.psum_pool(name="psum_h", bufs=4))
+
+        w_scales = keep.tile([P, E // PLANES, H], U8, align_bytes=64)
+        nc.vector.memset(w_scales[:].bitcast(I32), 0)
+
+        x_raw = []
+        for g in range(G):
+            raw = keep.tile([P, PACK, M], BF16, name="x_raw%d" % g)
+            nc.sync.dma_start(out=raw[:], in_=x[g].rearrange("(p j) m -> p j m", j=PACK))
+            x_raw.append(raw)
+        dm_raw = []
+        for g in range(G):
+            raw = keep.tile([P, PACK, SLOTS], BF16, name="dm_raw%d" % g)
+            nc.sync.dma_start(out=raw[:], in_=dispatch_mask[g].rearrange("(p j) e c -> p j (e c)", j=PACK))
+            dm_raw.append(raw)
+        for group in range(E // PLANES):
+            for quadrant in range(QUADRANTS):
+                nc.sync.dma_start(
+                    out=w_scales[32 * quadrant : 32 * quadrant + PLANES * 4, group, :].bitcast(I32),
+                    in_=wi_scales[
+                        PLANES * group : PLANES * (group + 1), 4 * quadrant : 4 * quadrant + 4, :
+                    ].bitcast(I32),
+                )
+        w_words = []
+        for pair in range(N_PAIRS):
+            words = keep.tile([P, PAIR, H], U32, name="w_words%d" % pair, align_bytes=64)
+            nc.sync.dma_start(
+                out=words[:].bitcast(I32),
+                in_=wi_words[PAIR * pair : PAIR * (pair + 1)].rearrange("e p n t -> p e (n t)").bitcast(I32),
+            )
+            w_words.append(words)
+
+        x_codes, x_scales, dm_codes, dm_scales = [], [], [], []
+        x_grouped, dm_grouped = [], []
+        for g in range(G):
+            grouped = keep.tile([P, PACK, P, PACK], BF16, name="x_grouped%d" % g, align_bytes=64)
+            nc.vector.tensor_copy(out=grouped[:], in_=x_raw[g][:].rearrange("p j (q t) -> p t q j", t=PACK))
+            x_grouped.append(grouped)
+        for g in range(G):
+            grouped = keep.tile([P, SLOTS, PACK], BF16, name="dm_grouped%d" % g, align_bytes=64)
+            nc.vector.tensor_copy(
+                out=grouped[:].rearrange("p (n i) j -> p n j i", i=4),
+                in_=dm_raw[g][:].rearrange("p j (n i) -> p n j i", i=4),
+            )
+            dm_grouped.append(grouped)
+            codes = keep.tile([P, M], U32, name="x_codes%d" % g, align_bytes=64)
+            scales = keep.tile([P, M], U8, name="x_scales%d" % g, align_bytes=64)
+            nc.vector.quantize_mx(
+                out=codes[:].bitcast(FP8X4),
+                scales=scales[:],
+                in_=x_grouped[g][:].rearrange("p t q j -> p (t q j)"),
+            )
+            x_codes.append(codes)
+            x_scales.append(scales)
+        for g in range(G):
+            codes = keep.tile([P, SLOTS], U32, name="dm_codes%d" % g, align_bytes=64)
+            scales = keep.tile([P, SLOTS], U8, name="dm_scales%d" % g, align_bytes=64)
+            nc.vector.quantize_mx(
+                out=codes[:].bitcast(FP8X4),
+                scales=scales[:],
+                in_=dm_grouped[g][:].rearrange("p n j -> p (n j)"),
+            )
+            dm_codes.append(codes)
+            dm_scales.append(scales)
+
+        d_codes, d_scales = [], []
+
+        def dispatch(pair):
+            slots = slice(PAIR * C * pair, PAIR * C * (pair + 1))
+            grouped = keep.tile([P, PAIR, G, C, PACK], BF16, name="d_grouped%d" % pair, align_bytes=64)
+            for g in range(G):
+                bank = psum_d.tile([P, PACK, PAIR * C], F32, name="d_bank")
+                for t in range(PACK):
+                    m_cols = slice(P * t, P * (t + 1))
+                    nc.tensor.matmul_mx(
+                        out=bank[:, t, :],
+                        lhsT=x_codes[g][:, m_cols].bitcast(FP8X4),
+                        lhsT_scale=x_scales[g][:, m_cols],
+                        rhs=dm_codes[g][:, slots].bitcast(FP8X4),
+                        rhs_scale=dm_scales[g][:, slots],
+                        start=True,
+                        stop=True,
+                    )
+                nc.vector.tensor_copy(
+                    out=grouped[:, :, g, :, :], in_=bank[:].rearrange("p t (e c) -> p e c t", e=PAIR)
+                )
+            codes = keep.tile([P, PAIR * G * C], U32, name="d_codes%d" % pair, align_bytes=64)
+            scales = keep.tile([P, PAIR * G * C], U8, name="d_scales%d" % pair, align_bytes=64)
+            nc.vector.quantize_mx(
+                out=codes[:].bitcast(FP8X4),
+                scales=scales[:],
+                in_=grouped[:].rearrange("p e g c t -> p (e g c t)"),
+            )
+            d_codes.append(codes)
+            d_scales.append(scales)
+
+        def project(pair):
+            for i in range(PAIR):
+                e = PAIR * pair + i
+                rows = slice(G * C * i, G * C * (i + 1))
+                first_row = 4 * (e % PLANES)
+                h_sb = keep.tile([P, H], F32, name="h_sb%d" % e)
+                for n0 in range(0, H, BANK):
+                    h_bank = psum_h.tile([P, BANK], F32, name="h_bank")
+                    nc.tensor.matmul_mx(
+                        out=h_bank[:],
+                        lhsT=d_codes[pair][:, rows].bitcast(FP8X4),
+                        lhsT_scale=d_scales[pair][:, rows],
+                        rhs=w_words[pair][:, i, n0 : n0 + BANK].bitcast(FP8X4),
+                        rhs_scale=w_scales[first_row:P, e // PLANES, n0 : n0 + BANK],
+                        start=True,
+                        stop=True,
+                    )
+                    nc.scalar.activation(out=h_sb[:, n0 : n0 + BANK], in_=h_bank[:], func=RELU)
+                nc.sync.dma_start(out=out[e].rearrange("g c h -> (g c) h"), in_=h_sb[:])
+
+        dispatch(0)
+        for pair in range(1, N_PAIRS):
+            dispatch(pair)
+            project(pair - 1)
+        project(N_PAIRS - 1)

@@ -29,6 +29,7 @@ def tile_flaxpositionwisemoelayer_pa_e_kernel(tc, dispatch_mask, x, wi_words, wi
         keep = ctx.enter_context(tc.tile_pool(name="keep", bufs=1))
         psum_d = ctx.enter_context(tc.psum_pool(name="psum_d", bufs=4))
         psum_h = ctx.enter_context(tc.psum_pool(name="psum_h", bufs=4))
+        ctx.enter_context(tc.manual_schedule())
 
         w_scales = keep.tile([P, E // PLANES, H], U8, align_bytes=64)
         nc.vector.memset(w_scales[:].bitcast(I32), 0)

@@ -46,11 +46,11 @@ def tile_flaxpositionwisemoelayer_pa_e_kernel(tc, dispatch_mask, x, wi_words, wi
             dm_raw.append(raw)
         for group in range(E // PLANES):
             for quadrant in range(QUADRANTS):
-                nc.sync.dma_start(
-                    out=w_scales[32 * quadrant : 32 * quadrant + PLANES * 4, group, :].bitcast(I32),
+                nc.gpsimd.dma_start(
+                    out=w_scales[32 * quadrant : 32 * quadrant + PLANES * 4, group, :].bitcast(F32),
                     in_=wi_scales[
                         PLANES * group : PLANES * (group + 1), 4 * quadrant : 4 * quadrant + 4, :
-                    ].bitcast(I32),
+                    ].bitcast(F32),
                 )
         w_words = []
         for pair in range(N_PAIRS):

@@ -19,6 +19,7 @@ N_PAIRS = E // PAIR
 BANK = 512
 PLANES = 4
 QUADRANTS = 4
+DMA_ALIGN = 256
 
 FLOPS = 2 * G * S * SLOTS * M + 2 * E * G * C * M * H
 
@@ -31,18 +32,23 @@ def tile_flaxpositionwisemoelayer_pa_e_kernel(tc, dispatch_mask, x, wi_words, wi
         psum_h = ctx.enter_context(tc.psum_pool(name="psum_h", bufs=4))
         ctx.enter_context(tc.manual_schedule())
 
-        w_scales = keep.tile([P, E // PLANES, H], U8, align_bytes=64)
+        w_scales = keep.tile([P, E // PLANES, H], U8, align_bytes=DMA_ALIGN)
         nc.vector.memset(w_scales[:].bitcast(I32), 0)
 
         x_raw = []
         for g in range(G):
-            raw = keep.tile([P, PACK, M], BF16, name="x_raw%d" % g)
-            nc.sync.dma_start(out=raw[:], in_=x[g].rearrange("(p j) m -> p j m", j=PACK))
+            raw = keep.tile([P, PACK, M], BF16, name="x_raw%d" % g, align_bytes=DMA_ALIGN)
+            nc.sync.dma_start(
+                out=raw[:].rearrange("p j m -> p (j m)"), in_=x[g].rearrange("(p j) m -> p (j m)", j=PACK)
+            )
             x_raw.append(raw)
         dm_raw = []
         for g in range(G):
-            raw = keep.tile([P, PACK, SLOTS], BF16, name="dm_raw%d" % g)
-            nc.sync.dma_start(out=raw[:], in_=dispatch_mask[g].rearrange("(p j) e c -> p j (e c)", j=PACK))
+            raw = keep.tile([P, PACK, SLOTS], BF16, name="dm_raw%d" % g, align_bytes=DMA_ALIGN)
+            nc.sync.dma_start(
+                out=raw[:].rearrange("p j n -> p (j n)"),
+                in_=dispatch_mask[g].rearrange("(p j) e c -> p (j e c)", j=PACK),
+            )
             dm_raw.append(raw)
         for group in range(E // PLANES):
             for quadrant in range(QUADRANTS):
@@ -54,7 +60,7 @@ def tile_flaxpositionwisemoelayer_pa_e_kernel(tc, dispatch_mask, x, wi_words, wi
                 )
         w_words = []
         for pair in range(N_PAIRS):
-            words = keep.tile([P, PAIR, H], U32, name="w_words%d" % pair, align_bytes=64)
+            words = keep.tile([P, PAIR, H], U32, name="w_words%d" % pair, align_bytes=DMA_ALIGN)
             nc.sync.dma_start(
                 out=words[:].bitcast(I32),
                 in_=wi_words[PAIR * pair : PAIR * (pair + 1)].rearrange("e p n t -> p e (n t)").bitcast(I32),
@@ -130,7 +136,7 @@ def tile_flaxpositionwisemoelayer_pa_e_kernel(tc, dispatch_mask, x, wi_words, wi
                 e = PAIR * pair + i
                 rows = slice(G * C * i, G * C * (i + 1))
                 first_row = 4 * (e % PLANES)
-                h_sb = keep.tile([P, H], F32, name="h_sb%d" % e)
+                h_sb = keep.tile([P, H], F32, name="h_sb%d" % e, align_bytes=DMA_ALIGN)
                 for n0 in range(0, H, BANK):
                     h_bank = psum_h.tile([P, BANK], F32, name="h_bank")
                     nc.tensor.matmul_mx(

@@ -19,7 +19,7 @@ N_PAIRS = E // PAIR
 BANK = 512
 PLANES = 4
 QUADRANTS = 4
-DMA_ALIGN = 256
+DMA_ALIGN = 2048
 
 FLOPS = 2 * G * S * SLOTS * M + 2 * E * G * C * M * H
 
@@ -35,21 +35,17 @@ def tile_flaxpositionwisemoelayer_pa_e_kernel(tc, dispatch_mask, x, wi_words, wi
         w_scales = keep.tile([P, E // PLANES, H], U8, align_bytes=DMA_ALIGN)
         nc.vector.memset(w_scales[:].bitcast(I32), 0)
 
-        x_raw = []
+        x_raw = keep.tile([P, G, PACK, M], BF16, name="x_raw", align_bytes=DMA_ALIGN)
         for g in range(G):
-            raw = keep.tile([P, PACK, M], BF16, name="x_raw%d" % g, align_bytes=DMA_ALIGN)
             nc.sync.dma_start(
-                out=raw[:].rearrange("p j m -> p (j m)"), in_=x[g].rearrange("(p j) m -> p (j m)", j=PACK)
+                out=x_raw[:, g, :, :].rearrange("p j m -> p (j m)"), in_=x[g].rearrange("(p j) m -> p (j m)", j=PACK)
             )
-            x_raw.append(raw)
-        dm_raw = []
+        dm_raw = keep.tile([P, G, PACK, SLOTS], BF16, name="dm_raw", align_bytes=DMA_ALIGN)
         for g in range(G):
-            raw = keep.tile([P, PACK, SLOTS], BF16, name="dm_raw%d" % g, align_bytes=DMA_ALIGN)
             nc.sync.dma_start(
-                out=raw[:].rearrange("p j n -> p (j n)"),
+                out=dm_raw[:, g, :, :].rearrange("p j n -> p (j n)"),
                 in_=dispatch_mask[g].rearrange("(p j) e c -> p (j e c)", j=PACK),
             )
-            dm_raw.append(raw)
         for group in range(E // PLANES):
             for quadrant in range(QUADRANTS):
                 nc.gpsimd.dma_start(
@@ -58,26 +54,26 @@ def tile_flaxpositionwisemoelayer_pa_e_kernel(tc, dispatch_mask, x, wi_words, wi
                         PLANES * group : PLANES * (group + 1), 4 * quadrant : 4 * quadrant + 4, :
                     ].bitcast(F32),
                 )
-        w_words = []
+        w_words = keep.tile([P, E, H], U32, name="w_words", align_bytes=DMA_ALIGN)
         for pair in range(N_PAIRS):
-            words = keep.tile([P, PAIR, H], U32, name="w_words%d" % pair, align_bytes=DMA_ALIGN)
+            experts = slice(PAIR * pair, PAIR * (pair + 1))
             nc.sync.dma_start(
-                out=words[:].bitcast(I32),
-                in_=wi_words[PAIR * pair : PAIR * (pair + 1)].rearrange("e p n t -> p e (n t)").bitcast(I32),
+                out=w_words[:, experts, :].bitcast(I32),
+                in_=wi_words[experts].rearrange("e p n t -> p e (n t)").bitcast(I32),
             )
-            w_words.append(words)
+        h_sb = keep.tile([P, E, H], F32, name="h_sb", align_bytes=DMA_ALIGN)
 
         x_codes, x_scales, dm_codes, dm_scales = [], [], [], []
         x_grouped, dm_grouped = [], []
         for g in range(G):
             grouped = keep.tile([P, PACK, P, PACK], BF16, name="x_grouped%d" % g, align_bytes=64)
-            nc.vector.tensor_copy(out=grouped[:], in_=x_raw[g][:].rearrange("p j (q t) -> p t q j", t=PACK))
+            nc.vector.tensor_copy(out=grouped[:], in_=x_raw[:, g, :, :].rearrange("p j (q t) -> p t q j", t=PACK))
             x_grouped.append(grouped)
         for g in range(G):
             grouped = keep.tile([P, SLOTS, PACK], BF16, name="dm_grouped%d" % g, align_bytes=64)
             nc.vector.tensor_copy(
                 out=grouped[:].rearrange("p (n i) j -> p n j i", i=4),
-                in_=dm_raw[g][:].rearrange("p j (n i) -> p n j i", i=4),
+                in_=dm_raw[:, g, :, :].rearrange("p j (n i) -> p n j i", i=4),
             )
             dm_grouped.append(grouped)
             codes = keep.tile([P, M], U32, name="x_codes%d" % g, align_bytes=64)
@@ -136,20 +132,19 @@ def tile_flaxpositionwisemoelayer_pa_e_kernel(tc, dispatch_mask, x, wi_words, wi
                 e = PAIR * pair + i
                 rows = slice(G * C * i, G * C * (i + 1))
                 first_row = 4 * (e % PLANES)
-                h_sb = keep.tile([P, H], F32, name="h_sb%d" % e, align_bytes=DMA_ALIGN)
                 for n0 in range(0, H, BANK):
                     h_bank = psum_h.tile([P, BANK], F32, name="h_bank")
                     nc.tensor.matmul_mx(
                         out=h_bank[:],
                         lhsT=d_codes[pair][:, rows].bitcast(FP8X4),
                         lhsT_scale=d_scales[pair][:, rows],
-                        rhs=w_words[pair][:, i, n0 : n0 + BANK].bitcast(FP8X4),
+                        rhs=w_words[:, e, n0 : n0 + BANK].bitcast(FP8X4),
                         rhs_scale=w_scales[first_row:P, e // PLANES, n0 : n0 + BANK],
                         start=True,
                         stop=True,
                     )
-                    nc.scalar.activation(out=h_sb[:, n0 : n0 + BANK], in_=h_bank[:], func=RELU)
-                nc.sync.dma_start(out=out[e].rearrange("g c h -> (g c) h"), in_=h_sb[:])
+                    nc.scalar.activation(out=h_sb[:, e, n0 : n0 + BANK], in_=h_bank[:], func=RELU)
+                nc.sync.dma_start(out=out[e].rearrange("g c h -> (g c) h"), in_=h_sb[:, e, :])
 
         dispatch(0)
         for pair in range(1, N_PAIRS):

@@ -19,7 +19,8 @@ N_PAIRS = E // PAIR
 BANK = 512
 PLANES = 4
 QUADRANTS = 4
-DMA_ALIGN = 2048
+DMA_ALIGN = 256
+SHIFT = DMA_ALIGN // 2
 
 FLOPS = 2 * G * S * SLOTS * M + 2 * E * G * C * M * H
 
@@ -40,7 +41,8 @@ def tile_flaxpositionwisemoelayer_pa_e_kernel(tc, dispatch_mask, x, wi_words, wi
             nc.sync.dma_start(
                 out=x_raw[:, g, :, :].rearrange("p j m -> p (j m)"), in_=x[g].rearrange("(p j) m -> p (j m)", j=PACK)
             )
-        dm_raw = keep.tile([P, G, PACK, SLOTS], BF16, name="dm_raw", align_bytes=DMA_ALIGN)
+        dm_space = keep.tile([P, SHIFT // 2 + G * PACK * SLOTS], BF16, name="dm_space", align_bytes=DMA_ALIGN)
+        dm_raw = dm_space[:, SHIFT // 2 :].rearrange("p (g j n) -> p g j n", g=G, j=PACK)
         for g in range(G):
             nc.sync.dma_start(
                 out=dm_raw[:, g, :, :].rearrange("p j n -> p (j n)"),

from contextlib import ExitStack

import concourse.mybir as mybir

BF16 = mybir.dt.bfloat16
F32 = mybir.dt.float32
I32 = mybir.dt.int32
U32 = mybir.dt.uint32
U8 = mybir.dt.uint8
FP8X4 = mybir.dt.float8_e4m3fn_x4
RELU = mybir.ActivationFunctionType.Relu

G, S, M, H, E, C = 2, 512, 512, 1024, 16, 64
P = 128
PACK = 4
SLOTS = E * C
PAIR = 2
N_PAIRS = E // PAIR
BANK = 512
PLANES = 4
QUADRANTS = 4
DMA_ALIGN = 256
SHIFT = DMA_ALIGN // 2

FLOPS = 2 * G * S * SLOTS * M + 2 * E * G * C * M * H


def tile_flaxpositionwisemoelayer_pa_e_kernel(tc, dispatch_mask, x, wi_words, wi_scales, out):
    nc = tc.nc
    with ExitStack() as ctx:
        keep = ctx.enter_context(tc.tile_pool(name="keep", bufs=1))
        psum_d = ctx.enter_context(tc.psum_pool(name="psum_d", bufs=4))
        psum_h = ctx.enter_context(tc.psum_pool(name="psum_h", bufs=4))
        ctx.enter_context(tc.manual_schedule())

        w_scales = keep.tile([P, E // PLANES, H], U8, align_bytes=DMA_ALIGN)
        nc.vector.memset(w_scales[:].bitcast(I32), 0)

        x_raw = keep.tile([P, G, PACK, M], BF16, name="x_raw", align_bytes=DMA_ALIGN)
        for g in range(G):
            nc.sync.dma_start(
                out=x_raw[:, g, :, :].rearrange("p j m -> p (j m)"), in_=x[g].rearrange("(p j) m -> p (j m)", j=PACK)
            )
        dm_space = keep.tile([P, SHIFT // 2 + G * PACK * SLOTS], BF16, name="dm_space", align_bytes=DMA_ALIGN)
        dm_raw = dm_space[:, SHIFT // 2 :].rearrange("p (g j n) -> p g j n", g=G, j=PACK)
        for g in range(G):
            nc.sync.dma_start(
                out=dm_raw[:, g, :, :].rearrange("p j n -> p (j n)"),
                in_=dispatch_mask[g].rearrange("(p j) e c -> p (j e c)", j=PACK),
            )
        for group in range(E // PLANES):
            for quadrant in range(QUADRANTS):
                nc.gpsimd.dma_start(
                    out=w_scales[32 * quadrant : 32 * quadrant + PLANES * 4, group, :].bitcast(F32),
                    in_=wi_scales[
                        PLANES * group : PLANES * (group + 1), 4 * quadrant : 4 * quadrant + 4, :
                    ].bitcast(F32),
                )
        w_words = keep.tile([P, E, H], U32, name="w_words", align_bytes=DMA_ALIGN)
        for pair in range(N_PAIRS):
            experts = slice(PAIR * pair, PAIR * (pair + 1))
            nc.sync.dma_start(
                out=w_words[:, experts, :].bitcast(I32),
                in_=wi_words[experts].rearrange("e p n t -> p e (n t)").bitcast(I32),
            )
        h_sb = keep.tile([P, E, H], F32, name="h_sb", align_bytes=DMA_ALIGN)

        x_codes, x_scales, dm_codes, dm_scales = [], [], [], []
        x_grouped, dm_grouped = [], []
        for g in range(G):
            grouped = keep.tile([P, PACK, P, PACK], BF16, name="x_grouped%d" % g, align_bytes=64)
            nc.vector.tensor_copy(out=grouped[:], in_=x_raw[:, g, :, :].rearrange("p j (q t) -> p t q j", t=PACK))
            x_grouped.append(grouped)
        for g in range(G):
            grouped = keep.tile([P, SLOTS, PACK], BF16, name="dm_grouped%d" % g, align_bytes=64)
            nc.vector.tensor_copy(
                out=grouped[:].rearrange("p (n i) j -> p n j i", i=4),
                in_=dm_raw[:, g, :, :].rearrange("p j (n i) -> p n j i", i=4),
            )
            dm_grouped.append(grouped)
            codes = keep.tile([P, M], U32, name="x_codes%d" % g, align_bytes=64)
            scales = keep.tile([P, M], U8, name="x_scales%d" % g, align_bytes=64)
            nc.vector.quantize_mx(
                out=codes[:].bitcast(FP8X4),
                scales=scales[:],
                in_=x_grouped[g][:].rearrange("p t q j -> p (t q j)"),
            )
            x_codes.append(codes)
            x_scales.append(scales)
        for g in range(G):
            codes = keep.tile([P, SLOTS], U32, name="dm_codes%d" % g, align_bytes=64)
            scales = keep.tile([P, SLOTS], U8, name="dm_scales%d" % g, align_bytes=64)
            nc.vector.quantize_mx(
                out=codes[:].bitcast(FP8X4),
                scales=scales[:],
                in_=dm_grouped[g][:].rearrange("p n j -> p (n j)"),
            )
            dm_codes.append(codes)
            dm_scales.append(scales)

        d_codes, d_scales = [], []

        def dispatch(pair):
            slots = slice(PAIR * C * pair, PAIR * C * (pair + 1))
            grouped = keep.tile([P, PAIR, G, C, PACK], BF16, name="d_grouped%d" % pair, align_bytes=64)
            for g in range(G):
                bank = psum_d.tile([P, PACK, PAIR * C], F32, name="d_bank")
                for t in range(PACK):
                    m_cols = slice(P * t, P * (t + 1))
                    nc.tensor.matmul_mx(
                        out=bank[:, t, :],
                        lhsT=x_codes[g][:, m_cols].bitcast(FP8X4),
                        lhsT_scale=x_scales[g][:, m_cols],
                        rhs=dm_codes[g][:, slots].bitcast(FP8X4),
                        rhs_scale=dm_scales[g][:, slots],
                        start=True,
                        stop=True,
                    )
                nc.vector.tensor_copy(
                    out=grouped[:, :, g, :, :], in_=bank[:].rearrange("p t (e c) -> p e c t", e=PAIR)
                )
            codes = keep.tile([P, PAIR * G * C], U32, name="d_codes%d" % pair, align_bytes=64)
            scales = keep.tile([P, PAIR * G * C], U8, name="d_scales%d" % pair, align_bytes=64)
            nc.vector.quantize_mx(
                out=codes[:].bitcast(FP8X4),
                scales=scales[:],
                in_=grouped[:].rearrange("p e g c t -> p (e g c t)"),
            )
            d_codes.append(codes)
            d_scales.append(scales)

        def project(pair):
            for i in range(PAIR):
                e = PAIR * pair + i
                rows = slice(G * C * i, G * C * (i + 1))
                first_row = 4 * (e % PLANES)
                for n0 in range(0, H, BANK):
                    h_bank = psum_h.tile([P, BANK], F32, name="h_bank")
                    nc.tensor.matmul_mx(
                        out=h_bank[:],
                        lhsT=d_codes[pair][:, rows].bitcast(FP8X4),
                        lhsT_scale=d_scales[pair][:, rows],
                        rhs=w_words[:, e, n0 : n0 + BANK].bitcast(FP8X4),
                        rhs_scale=w_scales[first_row:P, e // PLANES, n0 : n0 + BANK],
                        start=True,
                        stop=True,
                    )
                    nc.scalar.activation(out=h_sb[:, e, n0 : n0 + BANK], in_=h_bank[:], func=RELU)
                nc.sync.dma_start(out=out[e].rearrange("g c h -> (g c) h"), in_=h_sb[:, e, :])

        dispatch(0)
        for pair in range(1, N_PAIRS):
            dispatch(pair)
            project(pair - 1)
        project(N_PAIRS - 1)
